import numpy as np
import ml_dtypes


def mxq(x, axis, fmt="e4m3"):
    dtype, down = {"e4m3": (ml_dtypes.float8_e4m3fn, 7), "e5m2": (ml_dtypes.float8_e5m2, 14)}[fmt]
    v = np.moveaxis(np.asarray(x, np.float32).astype(ml_dtypes.bfloat16).astype(np.float64), axis, -1)
    blocks = v.reshape(v.shape[:-1] + (-1, 32))
    amax = np.abs(blocks).max(-1, keepdims=True)
    byte = np.maximum(np.where(amax > 0, np.frexp(amax)[1] - 1 + 127, 0) - down, 1)
    scale = np.exp2(byte - 127.0)
    codes = (blocks / scale).astype(np.float32).astype(dtype).astype(np.float64)
    return np.moveaxis((codes * scale).reshape(v.shape), -1, axis)


WIDE = False


def mx_kscale(k):
    if not WIDE:
        return np.ones(k)
    levels = np.array([20, -20, 10, -10, 0])
    a = np.random.permutation(np.resize(levels, k // 512 * 4)).reshape(k // 512, 4)
    idx = np.arange(k)
    return np.exp2(a[idx // 512, idx % 128 // 32])


BF16 = ml_dtypes.bfloat16


def bf(x):
    return np.asarray(x, np.float32).astype(BF16)


def f64(x):
    return np.asarray(x).astype(np.float64)


B, CIN, COUT, T, F, KH, KW, PH, PW = 2, 128, 8192, 127, 2, 2, 3, 1, 1
OT = T + PH + PH - KH + 1


def setup_inputs():
    u = mx_kscale(COUT)
    x = np.random.standard_normal((B, CIN, T, F))
    kernel = np.random.standard_normal((COUT, CIN, F, KH, KW)) / np.sqrt(CIN * KH * KW) / u[:, None, None, None, None]
    bias = np.random.standard_normal((1, COUT, 1, F)) * 0.5
    g = np.random.standard_normal((B, COUT, OT, F)) * np.exp2(np.random.randint(-12, 1, (B, 1, OT, F))) * 16.0 * u[None, :, None, None]
    return {"x": bf(x), "kernel": bf(kernel), "bias": bf(bias), "grad_out": bf(g)}


def reference(x, kernel, bias, grad_out):
    gq = mxq(f64(grad_out).transpose(3, 2, 0, 1).reshape(F, OT * B, COUT), 2, "e5m2")
    kt = f64(kernel).transpose(2, 3, 4, 0, 1)
    gx = np.zeros((F, T * B, CIN))
    for m in range(KH):
        for n in range(KW):
            f0, f1 = max(0, PW - n), min(F, F + PW - n)
            t0, t1 = max(0, PH - m), min(OT, T + PH - m)
            p = gq[f0:f1] @ mxq(kt[f0:f1, m, n], 1, "e4m3")
            gx[f0 + n - PW:f1 + n - PW, (t0 + m - PH) * B:(t1 + m - PH) * B] += p[:, t0 * B:t1 * B]
    return np.ascontiguousarray(gx.reshape(F, T, B, CIN).transpose(2, 3, 1, 0))

@@ -1,0 +1,138 @@
+from contextlib import ExitStack
+
+import concourse.mybir as mybir
+from concourse.masks import make_identity
+
+BF16 = mybir.dt.bfloat16
+F32 = mybir.dt.float32
+U32 = mybir.dt.uint32
+U8 = mybir.dt.uint8
+E4M3_X4 = mybir.dt.float8_e4m3fn_x4
+E5M2_X4 = mybir.dt.float8_e5m2_x4
+
+B, CIN, COUT, T, F, KH, KW = 2, 128, 8192, 127, 2, 2, 3
+OT = T + 1
+P = 128
+PACK = 4
+K_PASS = P * PACK
+PASSES = COUT // K_PASS
+COLS = KH * CIN * F
+
+FLOPS = 2 * B * OT * COUT * F * COLS
+BYTES = 2 * COUT * CIN * F * KH * F + 2 * B * COUT * OT * F + 4 * B * CIN * T * F
+
+
+def load_pass(nc, raw, g_chunk, k_chunk):
+    g_raw = raw.tile([P, B, PACK, OT, F], BF16)
+    nc.sync.dma_start(out=g_raw[:].rearrange("p b j u y -> p b (j u y)"), in_=g_chunk)
+    k_raw = raw.tile([P, PACK, CIN, F * KH * KW], BF16)
+    nc.sync.dma_start(out=k_raw[:].rearrange("p j i s -> p (j i s)"), in_=k_chunk)
+    return g_raw, k_raw
+
+
+def regroup_pass(nc, grouped, g_raw, k_raw):
+    g_grouped = grouped.tile([P, B, F, OT, PACK], BF16, align_bytes=64)
+    nc.vector.tensor_copy(out=g_grouped[:], in_=g_raw[:].rearrange("p b j u y -> p b y u j"))
+
+    k_grouped = grouped.tile([P, F, KH, CIN, F, PACK], BF16, align_bytes=64)
+    for y in range(F):
+        for m in range(KH):
+            first = (y * KH + m) * KW + 1 - y
+            copy = nc.vector.tensor_copy if (y, m) == (0, 0) else nc.scalar.copy
+            copy(
+                out=k_grouped[:, y, m].rearrange("p i x j -> p i j x"),
+                in_=k_raw[:, :, :, first : first + F].rearrange("p j i x -> p i j x"),
+            )
+    return g_grouped, k_grouped
+
+
+def quantise_grad(nc, packed, g_grouped):
+    g_codes = packed.tile([P, B, F, OT], U32, align_bytes=64)
+    g_scales = packed.tile([P, B, F, OT], U8, align_bytes=64)
+    nc.vector.quantize_mx(
+        out=g_codes[:].rearrange("p b y u -> p (b y u)").bitcast(E5M2_X4),
+        scales=g_scales[:].rearrange("p b y u -> p (b y u)"),
+        in_=g_grouped[:].rearrange("p b y u j -> p (b y u j)"),
+    )
+    return g_codes, g_scales
+
+
+def quantise_kernel(nc, packed, k_grouped):
+    k_codes = packed.tile([P, F, COLS], U32, align_bytes=64)
+    k_scales = packed.tile([P, F, COLS], U8, align_bytes=64)
+    for y in range(F):
+        nc.vector.quantize_mx(
+            out=k_codes[:, y, :].bitcast(E4M3_X4),
+            scales=k_scales[:, y, :],
+            in_=k_grouped[:, y].rearrange("p m i x j -> p (m i x j)"),
+        )
+    return k_codes, k_scales
+
+
+def multiply_pass(nc, acc, c, g_codes, g_scales, k_codes, k_scales):
+    for y in range(F):
+        for b in range(B):
+            nc.tensor.matmul_mx(
+                out=acc[b][:].rearrange("p m i x -> p (m i x)"),
+                lhsT=g_codes[:, b, y, :].bitcast(E5M2_X4),
+                lhsT_scale=g_scales[:, b, y, :],
+                rhs=k_codes[:, y, :].bitcast(E4M3_X4),
+                rhs_scale=k_scales[:, y, :],
+                start=(c == 0 and y == 0),
+                stop=(c == PASSES - 1 and y == F - 1),
+            )
+
+
+def tile_svconv2d_pa_k_kernel(tc, x, kernel, bias, grad_out, out):
+    nc = tc.nc
+    g_chunks = grad_out.rearrange("b (c p j) u y -> c p b (j u y)", p=P, j=PACK)
+    k_chunks = kernel.rearrange("(c p j) i y m n -> c p (j i y m n)", p=P, j=PACK)
+
+    with ExitStack() as ctx:
+        raw = ctx.enter_context(tc.tile_pool(name="raw", bufs=4))
+        grouped = ctx.enter_context(tc.tile_pool(name="grouped", bufs=3))
+        packed = ctx.enter_context(tc.tile_pool(name="packed", bufs=3))
+        tail = ctx.enter_context(tc.tile_pool(name="tail", bufs=1))
+        psum = ctx.enter_context(tc.psum_pool(name="psum", bufs=1))
+
+        identity = tail.tile([P, P], F32)
+        make_identity(nc, identity[:])
+
+        acc = [psum.tile([P, KH, CIN, F], F32, name="acc%d" % b) for b in range(B)]
+
+        waiting = None
+        for c in range(PASSES + 1):
+            if c < PASSES:
+                g_raw, k_raw = load_pass(nc, raw, g_chunks[c], k_chunks[c])
+                g_grouped, k_grouped = regroup_pass(nc, grouped, g_raw, k_raw)
+            if waiting is not None:
+                g_codes, g_scales = quantise_grad(nc, packed, waiting[0])
+                k_codes, k_scales = quantise_kernel(nc, packed, waiting[1])
+                multiply_pass(nc, acc, c - 1, g_codes, g_scales, k_codes, k_scales)
+            waiting = (g_grouped, k_grouped)
+
+        frames = [tail.tile([P, KH, F, CIN], F32, name="frames%d" % b) for b in range(B)]
+        nc.vector.tensor_copy(out=frames[0][:], in_=acc[0][:].rearrange("p m i x -> p m x i"))
+        nc.scalar.copy(out=frames[1][:], in_=acc[1][:].rearrange("p m i x -> p m x i"))
+
+        turned = [psum.tile([P, B, F, OT], F32, name="turned%d" % m) for m in range(KH)]
+        for b in range(B):
+            for m in range(KH):
+                for xb in range(F):
+                    nc.tensor.transpose(
+                        out=turned[m][:, b, xb, :], in_=frames[b][:, m, xb, :], identity=identity[:]
+                    )
+
+        early = tail.tile([P, B, T, F], F32)
+        nc.scalar.copy(out=early[:], in_=turned[0][:, :, :, 1:OT].rearrange("p b x t -> p b t x"))
+        result = tail.tile([P, B, T, F], F32)
+        nc.vector.tensor_tensor(
+            out=result[:],
+            in0=early[:],
+            in1=turned[1][:, :, :, 0:T].rearrange("p b x t -> p b t x"),
+            op=mybir.AluOpType.add,
+        )
+        nc.sync.dma_start(
+            out=out.rearrange("b i t x -> i b (t x)"),
+            in_=result[:].rearrange("p b t x -> p b (t x)"),
+        )

@@ -22,28 +22,35 @@ FLOPS = 2 * B * OT * COUT * F * COLS
 BYTES = 2 * COUT * CIN * F * KH * F + 2 * B * COUT * OT * F + 4 * B * CIN * T * F
 
 
-def load_pass(nc, raw, g_chunk, k_chunk):
+def load_grad(nc, raw, g_chunk):
     g_raw = raw.tile([P, B, PACK, OT, F], BF16)
     nc.sync.dma_start(out=g_raw[:].rearrange("p b j u y -> p b (j u y)"), in_=g_chunk)
+    return g_raw
+
+
+def load_kernel(nc, raw, k_chunk):
     k_raw = raw.tile([P, PACK, CIN, F * KH * KW], BF16)
     nc.sync.dma_start(out=k_raw[:].rearrange("p j i s -> p (j i s)"), in_=k_chunk)
-    return g_raw, k_raw
+    return k_raw
 
 
-def regroup_pass(nc, grouped, g_raw, k_raw):
+def regroup_grad(nc, grouped, g_raw):
     g_grouped = grouped.tile([P, B, F, OT, PACK], BF16, align_bytes=64)
     nc.vector.tensor_copy(out=g_grouped[:], in_=g_raw[:].rearrange("p b j u y -> p b y u j"))
+    return g_grouped
 
+
+def regroup_kernel(nc, grouped, k_raw, vector_pieces):
     k_grouped = grouped.tile([P, F, KH, CIN, F, PACK], BF16, align_bytes=64)
     for y in range(F):
         for m in range(KH):
             first = (y * KH + m) * KW + 1 - y
-            copy = nc.vector.tensor_copy if (y, m) == (0, 0) else nc.scalar.copy
+            copy = nc.vector.tensor_copy if y * KH + m < vector_pieces else nc.scalar.copy
             copy(
                 out=k_grouped[:, y, m].rearrange("p i x j -> p i j x"),
                 in_=k_raw[:, :, :, first : first + F].rearrange("p j i x -> p i j x"),
             )
-    return g_grouped, k_grouped
+    return k_grouped
 
 
 def quantise_grad(nc, packed, g_grouped):
@@ -57,30 +64,25 @@ def quantise_grad(nc, packed, g_grouped):
     return g_codes, g_scales
 
 
-def quantise_kernel(nc, packed, k_grouped):
-    k_codes = packed.tile([P, F, COLS], U32, align_bytes=64)
-    k_scales = packed.tile([P, F, COLS], U8, align_bytes=64)
-    for y in range(F):
-        nc.vector.quantize_mx(
-            out=k_codes[:, y, :].bitcast(E4M3_X4),
-            scales=k_scales[:, y, :],
-            in_=k_grouped[:, y].rearrange("p m i x j -> p (m i x j)"),
+def quantise_kernel(nc, k_codes, k_scales, k_grouped, y):
+    nc.vector.quantize_mx(
+        out=k_codes[:, y, :].bitcast(E4M3_X4),
+        scales=k_scales[:, y, :],
+        in_=k_grouped[:, y].rearrange("p m i x j -> p (m i x j)"),
+    )
+
+
+def multiply(nc, acc, c, y, g_codes, g_scales, k_codes, k_scales):
+    for b in range(B):
+        nc.tensor.matmul_mx(
+            out=acc[b][:].rearrange("p m i x -> p (m i x)"),
+            lhsT=g_codes[:, b, y, :].bitcast(E5M2_X4),
+            lhsT_scale=g_scales[:, b, y, :],
+            rhs=k_codes[:, y, :].bitcast(E4M3_X4),
+            rhs_scale=k_scales[:, y, :],
+            start=(c == 0 and y == 0),
+            stop=(c == PASSES - 1 and y == F - 1),
         )
-    return k_codes, k_scales
-
-
-def multiply_pass(nc, acc, c, g_codes, g_scales, k_codes, k_scales):
-    for y in range(F):
-        for b in range(B):
-            nc.tensor.matmul_mx(
-                out=acc[b][:].rearrange("p m i x -> p (m i x)"),
-                lhsT=g_codes[:, b, y, :].bitcast(E5M2_X4),
-                lhsT_scale=g_scales[:, b, y, :],
-                rhs=k_codes[:, y, :].bitcast(E4M3_X4),
-                rhs_scale=k_scales[:, y, :],
-                start=(c == 0 and y == 0),
-                stop=(c == PASSES - 1 and y == F - 1),
-            )
 
 
 def tile_svconv2d_pa_k_kernel(tc, x, kernel, bias, grad_out, out):
@@ -89,50 +91,63 @@ def tile_svconv2d_pa_k_kernel(tc, x, kernel, bias, grad_out, out):
     k_chunks = kernel.rearrange("(c p j) i y m n -> c p (j i y m n)", p=P, j=PACK)
 
     with ExitStack() as ctx:
-        raw = ctx.enter_context(tc.tile_pool(name="raw", bufs=4))
+        raw = ctx.enter_context(tc.tile_pool(name="raw", bufs=6))
         grouped = ctx.enter_context(tc.tile_pool(name="grouped", bufs=3))
         packed = ctx.enter_context(tc.tile_pool(name="packed", bufs=3))
         tail = ctx.enter_context(tc.tile_pool(name="tail", bufs=1))
         psum = ctx.enter_context(tc.psum_pool(name="psum", bufs=1))
+        ctx.enter_context(tc.manual_schedule())
 
         identity = tail.tile([P, P], F32)
         make_identity(nc, identity[:])
 
         acc = [psum.tile([P, KH, CIN, F], F32, name="acc%d" % b) for b in range(B)]
 
-        waiting = None
-        for c in range(PASSES + 1):
-            if c < PASSES:
-                g_raw, k_raw = load_pass(nc, raw, g_chunks[c], k_chunks[c])
-                g_grouped, k_grouped = regroup_pass(nc, grouped, g_raw, k_raw)
-            if waiting is not None:
-                g_codes, g_scales = quantise_grad(nc, packed, waiting[0])
-                k_codes, k_scales = quantise_kernel(nc, packed, waiting[1])
-                multiply_pass(nc, acc, c - 1, g_codes, g_scales, k_codes, k_scales)
-            waiting = (g_grouped, k_grouped)
+        g_raw = load_grad(nc, raw, g_chunks[0])
+        g_grouped = regroup_grad(nc, grouped, g_raw)
+        g_next = quantise_grad(nc, packed, g_grouped)
+        for c in range(PASSES):
+            last = c == PASSES - 1
+            g_codes, g_scales = g_next
+            k_raw = load_kernel(nc, raw, k_chunks[c])
+            if not last:
+                g_raw = load_grad(nc, raw, g_chunks[c + 1])
+
+            k_grouped = regroup_kernel(nc, grouped, k_raw, 3 if last else 1)
+            if not last:
+                g_grouped = regroup_grad(nc, grouped, g_raw)
+
+            k_codes = packed.tile([P, F, COLS], U32, align_bytes=64)
+            k_scales = packed.tile([P, F, COLS], U8, align_bytes=64)
+            quantise_kernel(nc, k_codes, k_scales, k_grouped, 0)
+            multiply(nc, acc, c, 0, g_codes, g_scales, k_codes, k_scales)
+            if not last:
+                g_next = quantise_grad(nc, packed, g_grouped)
+            quantise_kernel(nc, k_codes, k_scales, k_grouped, 1)
+            multiply(nc, acc, c, 1, g_codes, g_scales, k_codes, k_scales)
 
         frames = [tail.tile([P, KH, F, CIN], F32, name="frames%d" % b) for b in range(B)]
-        nc.vector.tensor_copy(out=frames[0][:], in_=acc[0][:].rearrange("p m i x -> p m x i"))
-        nc.scalar.copy(out=frames[1][:], in_=acc[1][:].rearrange("p m i x -> p m x i"))
-
         turned = [psum.tile([P, B, F, OT], F32, name="turned%d" % m) for m in range(KH)]
-        for b in range(B):
-            for m in range(KH):
+        for m in range(KH):
+            nc.vector.tensor_copy(out=frames[0][:, m], in_=acc[0][:, m].rearrange("p i x -> p x i"))
+            nc.scalar.copy(out=frames[1][:, m], in_=acc[1][:, m].rearrange("p i x -> p x i"))
+            for b in range(B):
                 for xb in range(F):
                     nc.tensor.transpose(
                         out=turned[m][:, b, xb, :], in_=frames[b][:, m, xb, :], identity=identity[:]
                     )
 
         early = tail.tile([P, B, T, F], F32)
-        nc.scalar.copy(out=early[:], in_=turned[0][:, :, :, 1:OT].rearrange("p b x t -> p b t x"))
         result = tail.tile([P, B, T, F], F32)
-        nc.vector.tensor_tensor(
-            out=result[:],
-            in0=early[:],
-            in1=turned[1][:, :, :, 0:T].rearrange("p b x t -> p b t x"),
-            op=mybir.AluOpType.add,
-        )
-        nc.sync.dma_start(
-            out=out.rearrange("b i t x -> i b (t x)"),
-            in_=result[:].rearrange("p b t x -> p b (t x)"),
-        )
+        for b in range(B):
+            nc.scalar.copy(out=early[:, b], in_=turned[0][:, b, :, 1:OT].rearrange("p x t -> p t x"))
+            nc.vector.tensor_tensor(
+                out=result[:, b],
+                in0=early[:, b],
+                in1=turned[1][:, b, :, 0:T].rearrange("p x t -> p t x"),
+                op=mybir.AluOpType.add,
+            )
+            nc.sync.dma_start(
+                out=out[b].rearrange("i t x -> i (t x)"),
+                in_=result[:, b].rearrange("p t x -> p (t x)"),
+            )

@@ -96,7 +96,6 @@ def tile_svconv2d_pa_k_kernel(tc, x, kernel, bias, grad_out, out):
         packed = ctx.enter_context(tc.tile_pool(name="packed", bufs=3))
         tail = ctx.enter_context(tc.tile_pool(name="tail", bufs=1))
         psum = ctx.enter_context(tc.psum_pool(name="psum", bufs=1))
-        ctx.enter_context(tc.manual_schedule())
 
         identity = tail.tile([P, P], F32)
         make_identity(nc, identity[:])

@@ -1,7 +1,6 @@
 from contextlib import ExitStack
 
 import concourse.mybir as mybir
-from concourse.masks import make_identity
 
 BF16 = mybir.dt.bfloat16
 F32 = mybir.dt.float32
@@ -16,9 +15,8 @@ P = 128
 PACK = 4
 K_PASS = P * PACK
 PASSES = COUT // K_PASS
-COLS = KH * CIN * F
 
-FLOPS = 2 * B * OT * COUT * F * COLS
+FLOPS = 2 * B * OT * COUT * F * KH * CIN * F
 BYTES = 2 * COUT * CIN * F * KH * F + 2 * B * COUT * OT * F + 4 * B * CIN * T * F
 
 
@@ -28,67 +26,66 @@ def load_grad(nc, raw, g_chunk):
     return g_raw
 
 
-def load_kernel(nc, raw, k_chunk):
+def load_kernel(nc, raw, k_chunk, i_cuts):
     k_raw = raw.tile([P, PACK, CIN, F * KH * KW], BF16)
-    nc.sync.dma_start(out=k_raw[:].rearrange("p j i s -> p (j i s)"), in_=k_chunk)
+    for lo, hi in zip(i_cuts[:-1], i_cuts[1:]):
+        nc.sync.dma_start(out=k_raw[:, :, lo:hi, :], in_=k_chunk[:, :, lo:hi, :])
     return k_raw
 
 
 def regroup_grad(nc, grouped, g_raw):
-    g_grouped = grouped.tile([P, B, F, OT, PACK], BF16, align_bytes=64)
-    nc.vector.tensor_copy(out=g_grouped[:], in_=g_raw[:].rearrange("p b j u y -> p b y u j"))
+    g_grouped = grouped.tile([P, F, B, OT, PACK], BF16, align_bytes=64)
+    for b in range(B):
+        nc.vector.tensor_copy(
+            out=g_grouped[:, :, b].rearrange("p y u j -> p u j y"),
+            in_=g_raw[:, b].rearrange("p j u y -> p u j y"),
+        )
     return g_grouped
 
 
-def regroup_kernel(nc, grouped, k_raw, vector_pieces):
-    k_grouped = grouped.tile([P, F, KH, CIN, F, PACK], BF16, align_bytes=64)
+def regroup_kernel(copy, k_grouped, k_raw, y, m, lo, hi):
+    first = (y * KH + m) * KW + 1 - y
+    copy(
+        out=k_grouped[:, y, m, :, lo:hi, :].rearrange("p x i j -> p i j x"),
+        in_=k_raw[:, :, lo:hi, first : first + F].rearrange("p j i x -> p i j x"),
+    )
+
+
+def quantise_grad(nc, g_codes, g_scales, g_grouped):
     for y in range(F):
-        for m in range(KH):
-            first = (y * KH + m) * KW + 1 - y
-            copy = nc.vector.tensor_copy if y * KH + m < vector_pieces else nc.scalar.copy
-            copy(
-                out=k_grouped[:, y, m].rearrange("p i x j -> p i j x"),
-                in_=k_raw[:, :, :, first : first + F].rearrange("p j i x -> p i j x"),
-            )
-    return k_grouped
+        nc.vector.quantize_mx(
+            out=g_codes[:, 2 * y + 1, :].bitcast(E5M2_X4),
+            scales=g_scales[:, 2 * y + 1, :],
+            in_=g_grouped[:, y].rearrange("p b u j -> p (b u j)"),
+        )
 
 
-def quantise_grad(nc, packed, g_grouped):
-    g_codes = packed.tile([P, B, F, OT], U32, align_bytes=64)
-    g_scales = packed.tile([P, B, F, OT], U8, align_bytes=64)
+def quantise_kernel(nc, k_codes, k_scales, k_grouped, y, m_lo, m_hi):
     nc.vector.quantize_mx(
-        out=g_codes[:].rearrange("p b y u -> p (b y u)").bitcast(E5M2_X4),
-        scales=g_scales[:].rearrange("p b y u -> p (b y u)"),
-        in_=g_grouped[:].rearrange("p b y u j -> p (b y u j)"),
-    )
-    return g_codes, g_scales
-
-
-def quantise_kernel(nc, k_codes, k_scales, k_grouped, y):
-    nc.vector.quantize_mx(
-        out=k_codes[:, y, :].bitcast(E4M3_X4),
-        scales=k_scales[:, y, :],
-        in_=k_grouped[:, y].rearrange("p m i x j -> p (m i x j)"),
+        out=k_codes[:, y, m_lo:m_hi].rearrange("p m x i -> p (m x i)").bitcast(E4M3_X4),
+        scales=k_scales[:, y, m_lo:m_hi].rearrange("p m x i -> p (m x i)"),
+        in_=k_grouped[:, y, m_lo:m_hi].rearrange("p m x i j -> p (m x i j)"),
     )
 
 
-def multiply(nc, acc, c, y, g_codes, g_scales, k_codes, k_scales):
-    for b in range(B):
+def multiply(nc, acc, c, y, m, g_codes, g_scales, k_codes, k_scales):
+    for xb in range(F):
+        first = 2 * y + 1 - xb
         nc.tensor.matmul_mx(
-            out=acc[b][:].rearrange("p m i x -> p (m i x)"),
-            lhsT=g_codes[:, b, y, :].bitcast(E5M2_X4),
-            lhsT_scale=g_scales[:, b, y, :],
-            rhs=k_codes[:, y, :].bitcast(E4M3_X4),
-            rhs_scale=k_scales[:, y, :],
-            start=(c == 0 and y == 0),
-            stop=(c == PASSES - 1 and y == F - 1),
+            out=acc[m][:].rearrange("p x b u -> p (x b u)"),
+            lhsT=k_codes[:, y, m, xb, :].bitcast(E4M3_X4),
+            lhsT_scale=k_scales[:, y, m, xb, :],
+            rhs=g_codes[:, first : first + 2, :].rearrange("p s n -> p (s n)").bitcast(E5M2_X4),
+            rhs_scale=g_scales[:, first : first + 2, :].rearrange("p s n -> p (s n)"),
+            start=(c == 0 and y == 0 and xb == 0),
+            stop=(c == PASSES - 1 and y == F - 1 and xb == F - 1),
         )
 
 
 def tile_svconv2d_pa_k_kernel(tc, x, kernel, bias, grad_out, out):
     nc = tc.nc
     g_chunks = grad_out.rearrange("b (c p j) u y -> c p b (j u y)", p=P, j=PACK)
-    k_chunks = kernel.rearrange("(c p j) i y m n -> c p (j i y m n)", p=P, j=PACK)
+    k_chunks = kernel.rearrange("(c p j) i y m n -> c p j i (y m n)", p=P, j=PACK)
 
     with ExitStack() as ctx:
         raw = ctx.enter_context(tc.tile_pool(name="raw", bufs=6))
@@ -97,53 +94,62 @@ def tile_svconv2d_pa_k_kernel(tc, x, kernel, bias, grad_out, out):
         tail = ctx.enter_context(tc.tile_pool(name="tail", bufs=1))
         psum = ctx.enter_context(tc.psum_pool(name="psum", bufs=1))
 
-        identity = tail.tile([P, P], F32)
-        make_identity(nc, identity[:])
+        acc = [psum.tile([P, F, B, OT], F32, name="acc%d" % m) for m in range(KH)]
 
-        acc = [psum.tile([P, KH, CIN, F], F32, name="acc%d" % b) for b in range(B)]
+        blocks = 2 * F + 1
+        g_ring = []
+        for n in range(3):
+            g_codes = tail.tile([P, blocks, B * OT], U32, name="g_codes%d" % n, align_bytes=64)
+            g_scales = tail.tile([P, blocks, B * OT], U8, name="g_scales%d" % n, align_bytes=64)
+            nc.gpsimd.memset(g_codes[:, 0:blocks:2, :], 0)
+            nc.gpsimd.memset(g_scales[:, 0:blocks:2, :], 0)
+            g_ring.append((g_codes, g_scales))
 
         g_raw = load_grad(nc, raw, g_chunks[0])
         g_grouped = regroup_grad(nc, grouped, g_raw)
-        g_next = quantise_grad(nc, packed, g_grouped)
+        quantise_grad(nc, g_ring[0][0], g_ring[0][1], g_grouped)
         for c in range(PASSES):
             last = c == PASSES - 1
-            g_codes, g_scales = g_next
-            k_raw = load_kernel(nc, raw, k_chunks[c])
+            g_codes, g_scales = g_ring[c % 3]
+            pieces = (0, 96, 128) if last else (0, 128)
+            k_raw = load_kernel(nc, raw, k_chunks[c], pieces)
             if not last:
                 g_raw = load_grad(nc, raw, g_chunks[c + 1])
 
-            k_grouped = regroup_kernel(nc, grouped, k_raw, 3 if last else 1)
+            k_grouped = grouped.tile([P, F, KH, F, CIN, PACK], BF16, align_bytes=64)
+            for lo, hi in zip(pieces[:-1], pieces[1:]):
+                for m in range(KH):
+                    for y in range(F):
+                        on_vector = m == 0 if last else m + y == 0
+                        copy = nc.vector.tensor_copy if on_vector else nc.scalar.copy
+                        regroup_kernel(copy, k_grouped, k_raw, y, m, lo, hi)
             if not last:
                 g_grouped = regroup_grad(nc, grouped, g_raw)
 
-            k_codes = packed.tile([P, F, COLS], U32, align_bytes=64)
-            k_scales = packed.tile([P, F, COLS], U8, align_bytes=64)
-            quantise_kernel(nc, k_codes, k_scales, k_grouped, 0)
-            multiply(nc, acc, c, 0, g_codes, g_scales, k_codes, k_scales)
-            if not last:
-                g_next = quantise_grad(nc, packed, g_grouped)
-            quantise_kernel(nc, k_codes, k_scales, k_grouped, 1)
-            multiply(nc, acc, c, 1, g_codes, g_scales, k_codes, k_scales)
+            k_codes = packed.tile([P, F, KH, F, CIN], U32, align_bytes=64)
+            k_scales = packed.tile([P, F, KH, F, CIN], U8, align_bytes=64)
+            if last:
+                for m in range(KH):
+                    for y in range(F):
+                        quantise_kernel(nc, k_codes, k_scales, k_grouped, y, m, m + 1)
+                        multiply(nc, acc, c, y, m, g_codes, g_scales, k_codes, k_scales)
+            else:
+                quantise_kernel(nc, k_codes, k_scales, k_grouped, 0, 0, KH)
+                for m in range(KH):
+                    multiply(nc, acc, c, 0, m, g_codes, g_scales, k_codes, k_scales)
+                quantise_grad(nc, g_ring[(c + 1) % 3][0], g_ring[(c + 1) % 3][1], g_grouped)
+                quantise_kernel(nc, k_codes, k_scales, k_grouped, 1, 0, KH)
+                for m in range(KH):
+                    multiply(nc, acc, c, 1, m, g_codes, g_scales, k_codes, k_scales)
 
-        frames = [tail.tile([P, KH, F, CIN], F32, name="frames%d" % b) for b in range(B)]
-        turned = [psum.tile([P, B, F, OT], F32, name="turned%d" % m) for m in range(KH)]
-        for m in range(KH):
-            nc.vector.tensor_copy(out=frames[0][:, m], in_=acc[0][:, m].rearrange("p i x -> p x i"))
-            nc.scalar.copy(out=frames[1][:, m], in_=acc[1][:, m].rearrange("p i x -> p x i"))
-            for b in range(B):
-                for xb in range(F):
-                    nc.tensor.transpose(
-                        out=turned[m][:, b, xb, :], in_=frames[b][:, m, xb, :], identity=identity[:]
-                    )
-
-        early = tail.tile([P, B, T, F], F32)
+        early = tail.tile([P, F, B, T], F32)
         result = tail.tile([P, B, T, F], F32)
+        nc.scalar.copy(out=early[:], in_=acc[0][:, :, :, 1:OT])
         for b in range(B):
-            nc.scalar.copy(out=early[:, b], in_=turned[0][:, b, :, 1:OT].rearrange("p x t -> p t x"))
             nc.vector.tensor_tensor(
                 out=result[:, b],
-                in0=early[:, b],
-                in1=turned[1][:, b, :, 0:T].rearrange("p x t -> p t x"),
+                in0=early[:, :, b].rearrange("p x t -> p t x"),
+                in1=acc[1][:, :, b, 0:T].rearrange("p x t -> p t x"),
                 op=mybir.AluOpType.add,
             )
             nc.sync.dma_start(

@@ -15,21 +15,33 @@ P = 128
 PACK = 4
 K_PASS = P * PACK
 PASSES = COUT // K_PASS
+RUN = 16
+RING = 4
+
 
 FLOPS = 2 * B * OT * COUT * F * KH * CIN * F
 BYTES = 2 * COUT * CIN * F * KH * F + 2 * B * COUT * OT * F + 4 * B * CIN * T * F
 
 
-def load_grad(nc, raw, g_chunk):
-    g_raw = raw.tile([P, B, PACK, OT, F], BF16)
-    nc.sync.dma_start(out=g_raw[:].rearrange("p b j u y -> p b (j u y)"), in_=g_chunk)
-    return g_raw
+def load_grad(nc, raw, g_view, c, passes):
+    k, w = divmod(c, RUN // PACK)
+    rows = slice(w * PACK, (w + passes) * PACK)
+    g_raw = raw.tile([P, B, passes * PACK, OT, F], BF16, name="g_raw%d" % passes)
+    for d in range(2):
+        nc.sync.dma_start(
+            out=g_raw[d:P:2].rearrange("s b e u y -> s b (e u y)"),
+            in_=g_view[k, d, :, :, rows].rearrange("s b e u y -> s b (e u y)"),
+        )
+    return [g_raw[:, :, v * PACK : (v + 1) * PACK] for v in range(passes)]
 
 
-def load_kernel(nc, raw, k_chunk, i_cuts):
+def load_kernel(nc, raw, k_view, c, i_cuts):
+    k, w = divmod(c, RUN // PACK)
+    rows = slice(w * PACK, (w + 1) * PACK)
     k_raw = raw.tile([P, PACK, CIN, F * KH * KW], BF16)
     for lo, hi in zip(i_cuts[:-1], i_cuts[1:]):
-        nc.sync.dma_start(out=k_raw[:, :, lo:hi, :], in_=k_chunk[:, :, lo:hi, :])
+        for d in range(2):
+            nc.sync.dma_start(out=k_raw[d:P:2, :, lo:hi, :], in_=k_view[k, d, :, rows, lo:hi, :])
     return k_raw
 
 
@@ -84,11 +96,11 @@ def multiply(nc, acc, c, y, m, g_codes, g_scales, k_codes, k_scales):
 
 def tile_svconv2d_pa_k_kernel(tc, x, kernel, bias, grad_out, out):
     nc = tc.nc
-    g_chunks = grad_out.rearrange("b (c p j) u y -> c p b (j u y)", p=P, j=PACK)
-    k_chunks = kernel.rearrange("(c p j) i y m n -> c p j i (y m n)", p=P, j=PACK)
+    g_view = grad_out.rearrange("b (s k d e) u y -> k d s b e u y", k=4, d=2, e=RUN)
+    k_view = kernel.rearrange("(s k d e) i y m n -> k d s e i (y m n)", k=4, d=2, e=RUN)
 
     with ExitStack() as ctx:
-        raw = ctx.enter_context(tc.tile_pool(name="raw", bufs=6))
+        raw = ctx.enter_context(tc.tile_pool(name="raw", bufs=5))
         grouped = ctx.enter_context(tc.tile_pool(name="grouped", bufs=3))
         packed = ctx.enter_context(tc.tile_pool(name="packed", bufs=3))
         tail = ctx.enter_context(tc.tile_pool(name="tail", bufs=1))
@@ -96,35 +108,45 @@ def tile_svconv2d_pa_k_kernel(tc, x, kernel, bias, grad_out, out):
 
         acc = [psum.tile([P, F, B, OT], F32, name="acc%d" % m) for m in range(KH)]
 
+        warm = tail.tile([P, 2], F32)
+        nc.gpsimd.memset(warm[:, 0:1], 0.0)
+        nc.scalar.copy(out=warm[:, 1:2], in_=warm[:, 0:1])
+
         blocks = 2 * F + 1
         g_ring = []
-        for n in range(3):
+        for n in range(RING):
             g_codes = tail.tile([P, blocks, B * OT], U32, name="g_codes%d" % n, align_bytes=64)
             g_scales = tail.tile([P, blocks, B * OT], U8, name="g_scales%d" % n, align_bytes=64)
             nc.gpsimd.memset(g_codes[:, 0:blocks:2, :], 0)
             nc.gpsimd.memset(g_scales[:, 0:blocks:2, :], 0)
             g_ring.append((g_codes, g_scales))
 
-        g_raw = load_grad(nc, raw, g_chunks[0])
-        g_grouped = regroup_grad(nc, grouped, g_raw)
+        g_raws = load_grad(nc, raw, g_view, 0, 1)
+        g_grouped = regroup_grad(nc, grouped, g_raws[0])
         quantise_grad(nc, g_ring[0][0], g_ring[0][1], g_grouped)
         for c in range(PASSES):
             last = c == PASSES - 1
-            g_codes, g_scales = g_ring[c % 3]
+            g_codes, g_scales = g_ring[c % RING]
             pieces = (0, 96, 128) if last else (0, 128)
-            k_raw = load_kernel(nc, raw, k_chunks[c], pieces)
-            if not last:
-                g_raw = load_grad(nc, raw, g_chunks[c + 1])
+            k_raw = load_kernel(nc, raw, k_view, c, pieces)
+            if c == 0:
+                g_raws += load_grad(nc, raw, g_view, 1, 1)
+                g_raws += load_grad(nc, raw, g_view, 2, 2)
+                g_grouped = regroup_grad(nc, grouped, g_raws[1])
+                quantise_grad(nc, g_ring[1][0], g_ring[1][1], g_grouped)
+            elif c % 2 == 1 and c + 3 < PASSES:
+                g_raws += load_grad(nc, raw, g_view, c + 3, 2)
+            prepare = c + 2 < PASSES
 
             k_grouped = grouped.tile([P, F, KH, F, CIN, PACK], BF16, align_bytes=64)
             for lo, hi in zip(pieces[:-1], pieces[1:]):
                 for m in range(KH):
                     for y in range(F):
-                        on_vector = m == 0 if last else m + y == 0
+                        on_vector = m + y == 0 if prepare else m == 0
                         copy = nc.vector.tensor_copy if on_vector else nc.scalar.copy
                         regroup_kernel(copy, k_grouped, k_raw, y, m, lo, hi)
-            if not last:
-                g_grouped = regroup_grad(nc, grouped, g_raw)
+            if prepare:
+                g_grouped = regroup_grad(nc, grouped, g_raws[c + 2])
 
             k_codes = packed.tile([P, F, KH, F, CIN], U32, align_bytes=64)
             k_scales = packed.tile([P, F, KH, F, CIN], U8, align_bytes=64)
@@ -137,7 +159,8 @@ def tile_svconv2d_pa_k_kernel(tc, x, kernel, bias, grad_out, out):
                 quantise_kernel(nc, k_codes, k_scales, k_grouped, 0, 0, KH)
                 for m in range(KH):
                     multiply(nc, acc, c, 0, m, g_codes, g_scales, k_codes, k_scales)
-                quantise_grad(nc, g_ring[(c + 1) % 3][0], g_ring[(c + 1) % 3][1], g_grouped)
+                if prepare:
+                    quantise_grad(nc, g_ring[(c + 2) % RING][0], g_ring[(c + 2) % RING][1], g_grouped)
                 quantise_kernel(nc, k_codes, k_scales, k_grouped, 1, 0, KH)
                 for m in range(KH):
                     multiply(nc, acc, c, 1, m, g_codes, g_scales, k_codes, k_scales)

@@ -142,7 +142,7 @@ def tile_svconv2d_pa_k_kernel(tc, x, kernel, bias, grad_out, out):
             for lo, hi in zip(pieces[:-1], pieces[1:]):
                 for m in range(KH):
                     for y in range(F):
-                        on_vector = m + y == 0 if prepare else m == 0
+                        on_vector = m == 0 and (y == 0 or c % 2 == 1 or not prepare)
                         copy = nc.vector.tensor_copy if on_vector else nc.scalar.copy
                         regroup_kernel(copy, k_grouped, k_raw, y, m, lo, hi)
             if prepare:

@@ -45,14 +45,11 @@ def load_kernel(nc, raw, k_view, c, i_cuts):
     return k_raw
 
 
-def regroup_grad(nc, grouped, g_raw):
-    g_grouped = grouped.tile([P, F, B, OT, PACK], BF16, align_bytes=64)
-    for b in range(B):
-        nc.vector.tensor_copy(
-            out=g_grouped[:, :, b].rearrange("p y u j -> p u j y"),
-            in_=g_raw[:, b].rearrange("p j u y -> p u j y"),
-        )
-    return g_grouped
+def regroup_grad(nc, g_grouped, g_raw, b):
+    nc.vector.tensor_copy(
+        out=g_grouped[:, :, b].rearrange("p y u j -> p u j y"),
+        in_=g_raw[:, b].rearrange("p j u y -> p u j y"),
+    )
 
 
 def regroup_kernel(copy, k_grouped, k_raw, y, m, lo, hi):
@@ -122,7 +119,9 @@ def tile_svconv2d_pa_k_kernel(tc, x, kernel, bias, grad_out, out):
             g_ring.append((g_codes, g_scales))
 
         g_raws = load_grad(nc, raw, g_view, 0, 1)
-        g_grouped = regroup_grad(nc, grouped, g_raws[0])
+        g_grouped = grouped.tile([P, F, B, OT, PACK], BF16, align_bytes=64)
+        for b in range(B):
+            regroup_grad(nc, g_grouped, g_raws[0], b)
         quantise_grad(nc, g_ring[0][0], g_ring[0][1], g_grouped)
         for c in range(PASSES):
             last = c == PASSES - 1
@@ -132,7 +131,9 @@ def tile_svconv2d_pa_k_kernel(tc, x, kernel, bias, grad_out, out):
             if c == 0:
                 g_raws += load_grad(nc, raw, g_view, 1, 1)
                 g_raws += load_grad(nc, raw, g_view, 2, 2)
-                g_grouped = regroup_grad(nc, grouped, g_raws[1])
+                g_grouped = grouped.tile([P, F, B, OT, PACK], BF16, align_bytes=64)
+                for b in range(B):
+                    regroup_grad(nc, g_grouped, g_raws[1], b)
                 quantise_grad(nc, g_ring[1][0], g_ring[1][1], g_grouped)
             elif c % 2 == 1 and c + 3 < PASSES:
                 g_raws += load_grad(nc, raw, g_view, c + 3, 2)
@@ -146,24 +147,17 @@ def tile_svconv2d_pa_k_kernel(tc, x, kernel, bias, grad_out, out):
                         copy = nc.vector.tensor_copy if on_vector else nc.scalar.copy
                         regroup_kernel(copy, k_grouped, k_raw, y, m, lo, hi)
             if prepare:
-                g_grouped = regroup_grad(nc, grouped, g_raws[c + 2])
-
+                g_grouped = grouped.tile([P, F, B, OT, PACK], BF16, align_bytes=64)
             k_codes = packed.tile([P, F, KH, F, CIN], U32, align_bytes=64)
             k_scales = packed.tile([P, F, KH, F, CIN], U8, align_bytes=64)
-            if last:
-                for m in range(KH):
-                    for y in range(F):
-                        quantise_kernel(nc, k_codes, k_scales, k_grouped, y, m, m + 1)
-                        multiply(nc, acc, c, y, m, g_codes, g_scales, k_codes, k_scales)
-            else:
-                quantise_kernel(nc, k_codes, k_scales, k_grouped, 0, 0, KH)
-                for m in range(KH):
-                    multiply(nc, acc, c, 0, m, g_codes, g_scales, k_codes, k_scales)
-                if prepare:
+            for m in range(KH):
+                if m == 1 and prepare:
                     quantise_grad(nc, g_ring[(c + 2) % RING][0], g_ring[(c + 2) % RING][1], g_grouped)
-                quantise_kernel(nc, k_codes, k_scales, k_grouped, 1, 0, KH)
-                for m in range(KH):
-                    multiply(nc, acc, c, 1, m, g_codes, g_scales, k_codes, k_scales)
+                for y in range(F):
+                    if m == 0 and prepare:
+                        regroup_grad(nc, g_grouped, g_raws[c + 2], y)
+                    quantise_kernel(nc, k_codes, k_scales, k_grouped, y, m, m + 1)
+                    multiply(nc, acc, c, y, m, g_codes, g_scales, k_codes, k_scales)
 
         early = tail.tile([P, F, B, T], F32)
         result = tail.tile([P, B, T, F], F32)

@@ -16,7 +16,8 @@ PACK = 4
 K_PASS = P * PACK
 PASSES = COUT // K_PASS
 RUN = 16
-RING = 4
+LEAD = 4
+RING = LEAD + 2
 
 
 FLOPS = 2 * B * OT * COUT * F * KH * CIN * F
@@ -118,44 +119,65 @@ def tile_svconv2d_pa_k_kernel(tc, x, kernel, bias, grad_out, out):
             nc.gpsimd.memset(g_scales[:, 0:blocks:2, :], 0)
             g_ring.append((g_codes, g_scales))
 
-        g_raws = load_grad(nc, raw, g_view, 0, 1)
-        g_grouped = grouped.tile([P, F, B, OT, PACK], BF16, align_bytes=64)
-        for b in range(B):
-            regroup_grad(nc, g_grouped, g_raws[0], b)
-        quantise_grad(nc, g_ring[0][0], g_ring[0][1], g_grouped)
+        g_raws, g_groups = [], []
+
+        def prepare_half(c, b):
+            if b == 0:
+                g_grouped = grouped.tile([P, F, B, OT, PACK], BF16, align_bytes=64)
+                g_groups.append(g_grouped)
+            regroup_grad(nc, g_groups[c], g_raws[c], b)
+
+        def finish(c):
+            quantise_grad(nc, g_ring[c % RING][0], g_ring[c % RING][1], g_groups[c])
+
+        k_raws = []
+
+        def load_k(c):
+            k_raws.append(load_kernel(nc, raw, k_view, c, (0, 96, 128) if c == PASSES - 1 else (0, 128)))
+
+        def load_g(c, passes):
+            g_raws.extend(load_grad(nc, raw, g_view, c, passes))
+
+        def load_for(c):
+            if c % 2 == 0 and c + LEAD < PASSES:
+                load_g(c + LEAD, 2)
+            if c >= 2:
+                load_k(c)
+
+        load_g(0, 1)
+        load_k(0)
+        load_g(1, 1)
+        load_g(2, 2)
+        load_k(1)
+        load_for(0)
+        for c in range(LEAD):
+            prepare_half(c, 0)
+            prepare_half(c, 1)
+            finish(c)
         for c in range(PASSES):
             last = c == PASSES - 1
             g_codes, g_scales = g_ring[c % RING]
             pieces = (0, 96, 128) if last else (0, 128)
-            k_raw = load_kernel(nc, raw, k_view, c, pieces)
-            if c == 0:
-                g_raws += load_grad(nc, raw, g_view, 1, 1)
-                g_raws += load_grad(nc, raw, g_view, 2, 2)
-                g_grouped = grouped.tile([P, F, B, OT, PACK], BF16, align_bytes=64)
-                for b in range(B):
-                    regroup_grad(nc, g_grouped, g_raws[1], b)
-                quantise_grad(nc, g_ring[1][0], g_ring[1][1], g_grouped)
-            elif c % 2 == 1 and c + 3 < PASSES:
-                g_raws += load_grad(nc, raw, g_view, c + 3, 2)
-            prepare = c + 2 < PASSES
+            if c >= 1:
+                load_for(c)
+            k_raw = k_raws[c]
+            prepare = c + LEAD < PASSES
 
             k_grouped = grouped.tile([P, F, KH, F, CIN, PACK], BF16, align_bytes=64)
             for lo, hi in zip(pieces[:-1], pieces[1:]):
                 for m in range(KH):
                     for y in range(F):
-                        on_vector = m == 0 and (y == 0 or c % 2 == 1 or not prepare)
+                        on_vector = m == 0 and (y == 0 or not prepare)
                         copy = nc.vector.tensor_copy if on_vector else nc.scalar.copy
                         regroup_kernel(copy, k_grouped, k_raw, y, m, lo, hi)
-            if prepare:
-                g_grouped = grouped.tile([P, F, B, OT, PACK], BF16, align_bytes=64)
             k_codes = packed.tile([P, F, KH, F, CIN], U32, align_bytes=64)
             k_scales = packed.tile([P, F, KH, F, CIN], U8, align_bytes=64)
             for m in range(KH):
                 if m == 1 and prepare:
-                    quantise_grad(nc, g_ring[(c + 2) % RING][0], g_ring[(c + 2) % RING][1], g_grouped)
+                    finish(c + LEAD)
                 for y in range(F):
                     if m == 0 and prepare:
-                        regroup_grad(nc, g_grouped, g_raws[c + 2], y)
+                        prepare_half(c + LEAD, y)
                     quantise_kernel(nc, k_codes, k_scales, k_grouped, y, m, m + 1)
                     multiply(nc, acc, c, y, m, g_codes, g_scales, k_codes, k_scales)
 

@@ -17,7 +17,7 @@ K_PASS = P * PACK
 PASSES = COUT // K_PASS
 RUN = 16
 LEAD = 4
-RING = LEAD + 2
+RING = 10
 
 
 FLOPS = 2 * B * OT * COUT * F * KH * CIN * F
@@ -27,7 +27,7 @@ BYTES = 2 * COUT * CIN * F * KH * F + 2 * B * COUT * OT * F + 4 * B * CIN * T * 
 def load_grad(nc, raw, g_view, c, passes):
     k, w = divmod(c, RUN // PACK)
     rows = slice(w * PACK, (w + passes) * PACK)
-    g_raw = raw.tile([P, B, passes * PACK, OT, F], BF16, name="g_raw%d" % passes)
+    g_raw = raw.tile([P, B, passes * PACK, OT, F], BF16, name="g_raw%d" % passes, bufs=2 if passes == 4 else 1)
     for d in range(2):
         nc.sync.dma_start(
             out=g_raw[d:P:2].rearrange("s b e u y -> s b (e u y)"),
@@ -61,11 +61,15 @@ def regroup_kernel(copy, k_grouped, k_raw, y, m, lo, hi):
     )
 
 
-def quantise_grad(nc, g_codes, g_scales, g_grouped):
+def grad_block(c, y):
+    return 2 * (F * (c % RING) + y) + 1
+
+
+def quantise_grad(nc, g_codes, g_scales, c, g_grouped):
     for y in range(F):
         nc.vector.quantize_mx(
-            out=g_codes[:, 2 * y + 1, :].bitcast(E5M2_X4),
-            scales=g_scales[:, 2 * y + 1, :],
+            out=g_codes[:, grad_block(c, y), :].bitcast(E5M2_X4),
+            scales=g_scales[:, grad_block(c, y), :],
             in_=g_grouped[:, y].rearrange("p b u j -> p (b u j)"),
         )
 
@@ -80,7 +84,7 @@ def quantise_kernel(nc, k_codes, k_scales, k_grouped, y, m_lo, m_hi):
 
 def multiply(nc, acc, c, y, m, g_codes, g_scales, k_codes, k_scales):
     for xb in range(F):
-        first = 2 * y + 1 - xb
+        first = grad_block(c, y) - xb
         nc.tensor.matmul_mx(
             out=acc[m][:].rearrange("p x b u -> p (x b u)"),
             lhsT=k_codes[:, y, m, xb, :].bitcast(E4M3_X4),
@@ -110,14 +114,13 @@ def tile_svconv2d_pa_k_kernel(tc, x, kernel, bias, grad_out, out):
         nc.gpsimd.memset(warm[:, 0:1], 0.0)
         nc.scalar.copy(out=warm[:, 1:2], in_=warm[:, 0:1])
 
-        blocks = 2 * F + 1
-        g_ring = []
-        for n in range(RING):
-            g_codes = tail.tile([P, blocks, B * OT], U32, name="g_codes%d" % n, align_bytes=64)
-            g_scales = tail.tile([P, blocks, B * OT], U8, name="g_scales%d" % n, align_bytes=64)
-            nc.gpsimd.memset(g_codes[:, 0:blocks:2, :], 0)
-            nc.gpsimd.memset(g_scales[:, 0:blocks:2, :], 0)
-            g_ring.append((g_codes, g_scales))
+        blocks = 2 * F * RING + 1
+        g_codes = tail.tile([P, blocks, B * OT], U32, align_bytes=64)
+        g_scales = tail.tile([P, blocks, B * OT], U8, align_bytes=64)
+        half = F * RING
+        nc.vector.memset(g_codes[:, 0:half:2, :], 0)
+        nc.gpsimd.memset(g_scales[:, 0:blocks:2, :].bitcast(U32), 0)
+        nc.gpsimd.memset(g_codes[:, half:blocks:2, :], 0)
 
         g_raws, g_groups = [], []
 
@@ -128,7 +131,7 @@ def tile_svconv2d_pa_k_kernel(tc, x, kernel, bias, grad_out, out):
             regroup_grad(nc, g_groups[c], g_raws[c], b)
 
         def finish(c):
-            quantise_grad(nc, g_ring[c % RING][0], g_ring[c % RING][1], g_groups[c])
+            quantise_grad(nc, g_codes, g_scales, c, g_groups[c])
 
         k_raws = []
 
@@ -138,28 +141,22 @@ def tile_svconv2d_pa_k_kernel(tc, x, kernel, bias, grad_out, out):
         def load_g(c, passes):
             g_raws.extend(load_grad(nc, raw, g_view, c, passes))
 
-        def load_for(c):
-            if c % 2 == 0 and c + LEAD < PASSES:
-                load_g(c + LEAD, 2)
-            if c >= 2:
-                load_k(c)
-
         load_g(0, 1)
         load_k(0)
-        load_g(1, 1)
-        load_g(2, 2)
+        load_g(1, 3)
         load_k(1)
-        load_for(0)
+        load_g(4, 4)
         for c in range(LEAD):
             prepare_half(c, 0)
             prepare_half(c, 1)
             finish(c)
         for c in range(PASSES):
             last = c == PASSES - 1
-            g_codes, g_scales = g_ring[c % RING]
             pieces = (0, 96, 128) if last else (0, 128)
-            if c >= 1:
-                load_for(c)
+            if c >= 2:
+                load_k(c)
+            if c in (4, 8):
+                load_g(c + 4, 4)
             k_raw = k_raws[c]
             prepare = c + LEAD < PASSES
 

@@ -74,11 +74,11 @@ def quantise_grad(nc, g_codes, g_scales, c, g_grouped):
         )
 
 
-def quantise_kernel(nc, k_codes, k_scales, k_grouped, y, m_lo, m_hi):
+def quantise_kernel(nc, k_codes, k_scales, k_grouped, y, m, x_lo, x_hi):
     nc.vector.quantize_mx(
-        out=k_codes[:, y, m_lo:m_hi].rearrange("p m x i -> p (m x i)").bitcast(E4M3_X4),
-        scales=k_scales[:, y, m_lo:m_hi].rearrange("p m x i -> p (m x i)"),
-        in_=k_grouped[:, y, m_lo:m_hi].rearrange("p m x i j -> p (m x i j)"),
+        out=k_codes[:, y, m, x_lo:x_hi].rearrange("p x i -> p (x i)").bitcast(E4M3_X4),
+        scales=k_scales[:, y, m, x_lo:x_hi].rearrange("p x i -> p (x i)"),
+        in_=k_grouped[:, y, m, x_lo:x_hi].rearrange("p x i j -> p (x i j)"),
     )
 
 
@@ -164,7 +164,7 @@ def tile_svconv2d_pa_k_kernel(tc, x, kernel, bias, grad_out, out):
             for lo, hi in zip(pieces[:-1], pieces[1:]):
                 for m in range(KH):
                     for y in range(F):
-                        on_vector = m == 0 and (y == 0 or not prepare)
+                        on_vector = m == 0 and (y == 0 or c % 2 == 1 or not prepare)
                         copy = nc.vector.tensor_copy if on_vector else nc.scalar.copy
                         regroup_kernel(copy, k_grouped, k_raw, y, m, lo, hi)
             k_codes = packed.tile([P, F, KH, F, CIN], U32, align_bytes=64)
@@ -175,7 +175,11 @@ def tile_svconv2d_pa_k_kernel(tc, x, kernel, bias, grad_out, out):
                 for y in range(F):
                     if m == 0 and prepare:
                         prepare_half(c + LEAD, y)
-                    quantise_kernel(nc, k_codes, k_scales, k_grouped, y, m, m + 1)
+                    if last and m + y == 0:
+                        quantise_kernel(nc, k_codes, k_scales, k_grouped, y, m, 0, 1)
+                        quantise_kernel(nc, k_codes, k_scales, k_grouped, y, m, 1, F)
+                    else:
+                        quantise_kernel(nc, k_codes, k_scales, k_grouped, y, m, 0, F)
                     multiply(nc, acc, c, y, m, g_codes, g_scales, k_codes, k_scales)
 
         early = tail.tile([P, F, B, T], F32)

from contextlib import ExitStack

import concourse.mybir as mybir

BF16 = mybir.dt.bfloat16
F32 = mybir.dt.float32
U32 = mybir.dt.uint32
U8 = mybir.dt.uint8
E4M3_X4 = mybir.dt.float8_e4m3fn_x4
E5M2_X4 = mybir.dt.float8_e5m2_x4

B, CIN, COUT, T, F, KH, KW = 2, 128, 8192, 127, 2, 2, 3
OT = T + 1
P = 128
PACK = 4
K_PASS = P * PACK
PASSES = COUT // K_PASS
RUN = 16
LEAD = 4
RING = 10


FLOPS = 2 * B * OT * COUT * F * KH * CIN * F
BYTES = 2 * COUT * CIN * F * KH * F + 2 * B * COUT * OT * F + 4 * B * CIN * T * F


def load_grad(nc, raw, g_view, c, passes):
    k, w = divmod(c, RUN // PACK)
    rows = slice(w * PACK, (w + passes) * PACK)
    g_raw = raw.tile([P, B, passes * PACK, OT, F], BF16, name="g_raw%d" % passes, bufs=2 if passes == 4 else 1)
    for d in range(2):
        nc.sync.dma_start(
            out=g_raw[d:P:2].rearrange("s b e u y -> s b (e u y)"),
            in_=g_view[k, d, :, :, rows].rearrange("s b e u y -> s b (e u y)"),
        )
    return [g_raw[:, :, v * PACK : (v + 1) * PACK] for v in range(passes)]


def load_kernel(nc, raw, k_view, c, i_cuts):
    k, w = divmod(c, RUN // PACK)
    rows = slice(w * PACK, (w + 1) * PACK)
    k_raw = raw.tile([P, PACK, CIN, F * KH * KW], BF16)
    for lo, hi in zip(i_cuts[:-1], i_cuts[1:]):
        for d in range(2):
            nc.sync.dma_start(out=k_raw[d:P:2, :, lo:hi, :], in_=k_view[k, d, :, rows, lo:hi, :])
    return k_raw


def regroup_grad(nc, g_grouped, g_raw, b):
    nc.vector.tensor_copy(
        out=g_grouped[:, :, b].rearrange("p y u j -> p u j y"),
        in_=g_raw[:, b].rearrange("p j u y -> p u j y"),
    )


def regroup_kernel(copy, k_grouped, k_raw, y, m, lo, hi):
    first = (y * KH + m) * KW + 1 - y
    copy(
        out=k_grouped[:, y, m, :, lo:hi, :].rearrange("p x i j -> p i j x"),
        in_=k_raw[:, :, lo:hi, first : first + F].rearrange("p j i x -> p i j x"),
    )


def grad_block(c, y):
    return 2 * (F * (c % RING) + y) + 1


def quantise_grad(nc, g_codes, g_scales, c, g_grouped):
    for y in range(F):
        nc.vector.quantize_mx(
            out=g_codes[:, grad_block(c, y), :].bitcast(E5M2_X4),
            scales=g_scales[:, grad_block(c, y), :],
            in_=g_grouped[:, y].rearrange("p b u j -> p (b u j)"),
        )


def quantise_kernel(nc, k_codes, k_scales, k_grouped, y, m, x_lo, x_hi):
    nc.vector.quantize_mx(
        out=k_codes[:, y, m, x_lo:x_hi].rearrange("p x i -> p (x i)").bitcast(E4M3_X4),
        scales=k_scales[:, y, m, x_lo:x_hi].rearrange("p x i -> p (x i)"),
        in_=k_grouped[:, y, m, x_lo:x_hi].rearrange("p x i j -> p (x i j)"),
    )


def multiply(nc, acc, c, y, m, g_codes, g_scales, k_codes, k_scales):
    for xb in range(F):
        first = grad_block(c, y) - xb
        nc.tensor.matmul_mx(
            out=acc[m][:].rearrange("p x b u -> p (x b u)"),
            lhsT=k_codes[:, y, m, xb, :].bitcast(E4M3_X4),
            lhsT_scale=k_scales[:, y, m, xb, :],
            rhs=g_codes[:, first : first + 2, :].rearrange("p s n -> p (s n)").bitcast(E5M2_X4),
            rhs_scale=g_scales[:, first : first + 2, :].rearrange("p s n -> p (s n)"),
            start=(c == 0 and y == 0 and xb == 0),
            stop=(c == PASSES - 1 and y == F - 1 and xb == F - 1),
        )


def tile_svconv2d_pa_k_kernel(tc, x, kernel, bias, grad_out, out):
    nc = tc.nc
    g_view = grad_out.rearrange("b (s k d e) u y -> k d s b e u y", k=4, d=2, e=RUN)
    k_view = kernel.rearrange("(s k d e) i y m n -> k d s e i (y m n)", k=4, d=2, e=RUN)

    with ExitStack() as ctx:
        raw = ctx.enter_context(tc.tile_pool(name="raw", bufs=5))
        grouped = ctx.enter_context(tc.tile_pool(name="grouped", bufs=3))
        packed = ctx.enter_context(tc.tile_pool(name="packed", bufs=3))
        tail = ctx.enter_context(tc.tile_pool(name="tail", bufs=1))
        psum = ctx.enter_context(tc.psum_pool(name="psum", bufs=1))

        acc = [psum.tile([P, F, B, OT], F32, name="acc%d" % m) for m in range(KH)]

        warm = tail.tile([P, 2], F32)
        nc.gpsimd.memset(warm[:, 0:1], 0.0)
        nc.scalar.copy(out=warm[:, 1:2], in_=warm[:, 0:1])

        blocks = 2 * F * RING + 1
        g_codes = tail.tile([P, blocks, B * OT], U32, align_bytes=64)
        g_scales = tail.tile([P, blocks, B * OT], U8, align_bytes=64)
        half = F * RING
        nc.vector.memset(g_codes[:, 0:half:2, :], 0)
        nc.gpsimd.memset(g_scales[:, 0:blocks:2, :].bitcast(U32), 0)
        nc.gpsimd.memset(g_codes[:, half:blocks:2, :], 0)

        g_raws, g_groups = [], []

        def prepare_half(c, b):
            if b == 0:
                g_grouped = grouped.tile([P, F, B, OT, PACK], BF16, align_bytes=64)
                g_groups.append(g_grouped)
            regroup_grad(nc, g_groups[c], g_raws[c], b)

        def finish(c):
            quantise_grad(nc, g_codes, g_scales, c, g_groups[c])

        k_raws = []

        def load_k(c):
            k_raws.append(load_kernel(nc, raw, k_view, c, (0, 96, 128) if c == PASSES - 1 else (0, 128)))

        def load_g(c, passes):
            g_raws.extend(load_grad(nc, raw, g_view, c, passes))

        load_g(0, 1)
        load_k(0)
        load_g(1, 3)
        load_k(1)
        load_g(4, 4)
        for c in range(LEAD):
            prepare_half(c, 0)
            prepare_half(c, 1)
            finish(c)
        for c in range(PASSES):
            last = c == PASSES - 1
            pieces = (0, 96, 128) if last else (0, 128)
            if c >= 2:
                load_k(c)
            if c in (4, 8):
                load_g(c + 4, 4)
            k_raw = k_raws[c]
            prepare = c + LEAD < PASSES

            k_grouped = grouped.tile([P, F, KH, F, CIN, PACK], BF16, align_bytes=64)
            for lo, hi in zip(pieces[:-1], pieces[1:]):
                for m in range(KH):
                    for y in range(F):
                        on_vector = m == 0 and (y == 0 or c % 2 == 1 or not prepare)
                        copy = nc.vector.tensor_copy if on_vector else nc.scalar.copy
                        regroup_kernel(copy, k_grouped, k_raw, y, m, lo, hi)
            k_codes = packed.tile([P, F, KH, F, CIN], U32, align_bytes=64)
            k_scales = packed.tile([P, F, KH, F, CIN], U8, align_bytes=64)
            for m in range(KH):
                if m == 1 and prepare:
                    finish(c + LEAD)
                for y in range(F):
                    if m == 0 and prepare:
                        prepare_half(c + LEAD, y)
                    if last and m + y == 0:
                        quantise_kernel(nc, k_codes, k_scales, k_grouped, y, m, 0, 1)
                        quantise_kernel(nc, k_codes, k_scales, k_grouped, y, m, 1, F)
                    else:
                        quantise_kernel(nc, k_codes, k_scales, k_grouped, y, m, 0, F)
                    multiply(nc, acc, c, y, m, g_codes, g_scales, k_codes, k_scales)

        early = tail.tile([P, F, B, T], F32)
        result = tail.tile([P, B, T, F], F32)
        nc.scalar.copy(out=early[:], in_=acc[0][:, :, :, 1:OT])
        for b in range(B):
            nc.vector.tensor_tensor(
                out=result[:, b],
                in0=early[:, :, b].rearrange("p x t -> p t x"),
                in1=acc[1][:, :, b, 0:T].rearrange("p x t -> p t x"),
                op=mybir.AluOpType.add,
            )
            nc.sync.dma_start(
                out=out[b].rearrange("i t x -> i (t x)"),
                in_=result[:, b].rearrange("p t x -> p (t x)"),
            )
